import numpy as np
import ml_dtypes


def mxq(x, axis, fmt="e4m3"):
    dtype, down = {"e4m3": (ml_dtypes.float8_e4m3fn, 7), "e5m2": (ml_dtypes.float8_e5m2, 14)}[fmt]
    v = np.moveaxis(np.asarray(x, np.float32).astype(ml_dtypes.bfloat16).astype(np.float64), axis, -1)
    blocks = v.reshape(v.shape[:-1] + (-1, 32))
    amax = np.abs(blocks).max(-1, keepdims=True)
    byte = np.maximum(np.where(amax > 0, np.frexp(amax)[1] - 1 + 127, 0) - down, 1)
    scale = np.exp2(byte - 127.0)
    codes = (blocks / scale).astype(np.float32).astype(dtype).astype(np.float64)
    return np.moveaxis((codes * scale).reshape(v.shape), -1, axis)


WIDE = False


def mx_kscale(k):
    if not WIDE:
        return np.ones(k)
    levels = np.array([20, -20, 10, -10, 0])
    a = np.random.permutation(np.resize(levels, k // 512 * 4)).reshape(k // 512, 4)
    idx = np.arange(k)
    return np.exp2(a[idx // 512, idx % 128 // 32])


BF16 = ml_dtypes.bfloat16


def bf(x):
    return np.asarray(x, np.float32).astype(BF16)


def f64(x):
    return np.asarray(x).astype(np.float64)


B, L, F, A = 512, 3, 2048, 512


def setup_inputs():
    u = mx_kscale(A)
    x = np.random.standard_normal((B, L, F))
    W = np.random.standard_normal((L, L, F, A)) * 0.016 / u
    g = np.random.standard_normal((B, L, A)) * np.exp2(np.random.randint(-12, 1, (B, L, 1))) * 8.0 * u
    return {"x": bf(x), "W": bf(W), "grad_out": bf(g)}


def reference(x, W, grad_out):
    n = W.shape[0]
    gq = mxq(f64(grad_out), 2, "e5m2")
    Wq = {(i, j): mxq(f64(W[i, j]), 1, "e4m3") for i in range(n) for j in range(i + 1)}
    cols = []
    for j in range(n):
        acc = 0.0
        for i in range(j, n):
            acc = acc + (gq[:, i, :] @ Wq[i, j].T)
        cols.append(acc)
    return np.stack(cols, axis=1)

@@ -1,0 +1,154 @@
+from contextlib import ExitStack
+
+import concourse.mybir as mybir
+from concourse.masks import make_identity
+
+F32 = mybir.dt.float32
+BF16 = mybir.dt.bfloat16
+U32 = mybir.dt.uint32
+U8 = mybir.dt.uint8
+E4X4 = mybir.dt.float8_e4m3fn_x4
+E5X4 = mybir.dt.float8_e5m2_x4
+
+P = 128
+B, L, F, A = 512, 3, 2048, 512
+NT = B // P
+CH = 512
+NQ = F // CH
+FLOPS = 2 * B * A * F * 6
+BYTES = 6 * F * A * 2 + B * L * A * 2 + B * L * F * 4
+
+
+def tile_decoder_kernel(tc, x, W, grad_out, out):
+    nc = tc.nc
+    with ExitStack() as ctx:
+        ctx.enter_context(tc.manual_schedule())
+        const = ctx.enter_context(tc.tile_pool(name="const", bufs=1))
+        rawp = ctx.enter_context(tc.tile_pool(name="rawp", bufs=6))
+        grp = ctx.enter_context(tc.tile_pool(name="grp", bufs=4))
+        cod = ctx.enter_context(tc.tile_pool(name="cod", bufs=12))
+        outp = ctx.enter_context(tc.tile_pool(name="outp", bufs=24))
+        psum = ctx.enter_context(tc.psum_pool(name="psum", bufs=8))
+
+        ident = const.tile([P, P], F32, name="ident")
+        make_identity(nc, ident[:])
+
+        gv = grad_out.rearrange("(p t) i a -> p t i a", t=NT)
+        ov = out.rearrange("(m t) j f -> m t j f", t=NT)
+
+        src = {}
+        g2raw = const.tile([P, NT * A], BF16, name="g2raw")
+        nc.sync.dma_start(out=g2raw[:].rearrange("p (t a) -> p t a", t=NT), in_=gv[:, :, 2, :])
+        src[("g", 2)] = (g2raw[:].bitcast(F32), 0, A // 2)
+
+        def load_w(i, j, q0, nq, pool, tag):
+            raw = pool.tile([P, nq * 4 * A], BF16, name="raw%d%d%d" % (i, j, q0), tag=tag)
+            wv = W[i, j].rearrange("(q p t) a -> p q (t a)", p=P, t=4)
+            nc.sync.dma_start(out=raw[:].rearrange("p (q x) -> p q x", q=nq), in_=wv[:, q0 : q0 + nq, :])
+            for c in range(nq):
+                src[(i, j, q0 + c)] = (raw[:].bitcast(F32), c * 2 * A, A // 2)
+
+        load_w(2, 2, 0, 1, const, "rawh0")
+        load_w(2, 2, 1, 1, const, "rawh1")
+        load_w(2, 2, 2, 2, rawp, "raw")
+        g01raw = const.tile([P, NT * 2 * A], BF16, name="g01raw")
+        nc.sync.dma_start(
+            out=g01raw[:].rearrange("p (t i a) -> p t i a", t=NT, i=2), in_=gv[:, :, 0:2, :]
+        )
+        for i in range(2):
+            src[("g", i)] = (g01raw[:].bitcast(F32), i * (A // 2), A)
+        for j, h in ((1, 0), (1, 1), (0, 0), (0, 1)):
+            for i in range(j, L):
+                load_w(i, j, 2 * h, 2, rawp, "raw")
+
+        count = {"tc": 0, "ev": 0}
+        grouped = {}
+        codes = {}
+
+        def copy_out(turn_vector, dst, srcv):
+            if turn_vector:
+                nc.vector.tensor_copy(out=dst, in_=srcv)
+            else:
+                nc.scalar.copy(out=dst, in_=srcv)
+
+        def transpose_chunk(key):
+            words, col0, step = src[key]
+            g = grp.tile([P, 4 * CH], BF16, name="grouped", align_bytes=64)
+            grouped[key] = g
+            gf = g[:].bitcast(F32)
+            for h in range(2):
+                xt = psum.tile([P, 512], F32, name="xt", tag="bank")
+                for u in range(2):
+                    for s in range(2):
+                        c = col0 + (2 * h + s) * step + u * P
+                        nc.tensor.transpose(
+                            xt[:, u * 256 + s * P : u * 256 + (s + 1) * P], words[:, c : c + P], ident[:]
+                        )
+                copy_out(
+                    count["tc"] % 4 == 3,
+                    gf[:, h * 512 : (h + 1) * 512].rearrange("p (c u) -> p c u", u=2),
+                    xt[:].rearrange("p (u c) -> p c u", u=2),
+                )
+                count["tc"] += 1
+
+        def quantise_chunk(key):
+            if key[0] == "g":
+                cw = const.tile([P, CH], U32, name="gcodes%d" % key[1], align_bytes=64)
+                sc = const.tile([P, CH], U8, name="gscale%d" % key[1], align_bytes=64)
+                fmt = E5X4
+            else:
+                cw = cod.tile([P, CH], U32, name="wcodes", align_bytes=64)
+                sc = cod.tile([P, CH], U8, name="wscale", align_bytes=64)
+                fmt = E4X4
+            nc.vector.quantize_mx(out=cw[:].bitcast(fmt), scales=sc[:], in_=grouped[key][:])
+            codes[key] = (cw, sc)
+
+        def run_t(keys):
+            prev = None
+            for key in keys:
+                transpose_chunk(key)
+                if prev is not None:
+                    quantise_chunk(prev)
+                prev = key
+            quantise_chunk(prev)
+
+        def keys_of(j, h):
+            return [(i, j, q) for q in (2 * h, 2 * h + 1) for i in range(j, L)]
+
+        def run_m(j, h):
+            for t in range(NT):
+                ot = outp.tile([P, 2 * CH], F32, name="ot")
+                for c in range(2):
+                    acc = psum.tile([P, 512], F32, name="acc", tag="bank")
+                    for i in range(j, L):
+                        gc, gs = codes[("g", i)]
+                        wc, ws = codes[(i, j, 2 * h + c)]
+                        nc.tensor.matmul_mx(
+                            out=acc[:],
+                            lhsT=gc[:, t * P : (t + 1) * P].bitcast(E5X4),
+                            lhsT_scale=gs[:, t * P : (t + 1) * P],
+                            rhs=wc[:].bitcast(E4X4),
+                            rhs_scale=ws[:],
+                            start=(i == j),
+                            stop=(i == L - 1),
+                        )
+                    copy_out(
+                        count["ev"] % 2 == 1,
+                        ot[:, c * CH : (c + 1) * CH].rearrange("p (f s) -> p f s", s=4),
+                        acc[:].rearrange("p (s f) -> p f s", s=4),
+                    )
+                    count["ev"] += 1
+                nc.sync.dma_start(out=ov[:, t, j, h * 2 * CH : (h + 1) * 2 * CH], in_=ot[:])
+
+        run_t([("g", 2)] + keys_of(2, 0))
+        run_t(keys_of(2, 1))
+        run_m(2, 0)
+        run_t([("g", 1), ("g", 0)] + keys_of(1, 0))
+        run_m(2, 1)
+        run_t(keys_of(1, 1))
+        run_m(1, 0)
+        run_t(keys_of(0, 0))
+        run_m(1, 1)
+        run_t(keys_of(0, 1))
+        run_m(0, 0)
+        run_m(0, 1)

@@ -27,7 +27,7 @@ def tile_decoder_kernel(tc, x, W, grad_out, out):
         rawp = ctx.enter_context(tc.tile_pool(name="rawp", bufs=6))
         grp = ctx.enter_context(tc.tile_pool(name="grp", bufs=4))
         cod = ctx.enter_context(tc.tile_pool(name="cod", bufs=12))
-        outp = ctx.enter_context(tc.tile_pool(name="outp", bufs=24))
+        outp = ctx.enter_context(tc.tile_pool(name="outp", bufs=12))
         psum = ctx.enter_context(tc.psum_pool(name="psum", bufs=8))
 
         ident = const.tile([P, P], F32, name="ident")
@@ -43,21 +43,23 @@ def tile_decoder_kernel(tc, x, W, grad_out, out):
 
         def load_w(i, j, q0, nq, pool, tag):
             raw = pool.tile([P, nq * 4 * A], BF16, name="raw%d%d%d" % (i, j, q0), tag=tag)
-            wv = W[i, j].rearrange("(q p t) a -> p q (t a)", p=P, t=4)
-            nc.sync.dma_start(out=raw[:].rearrange("p (q x) -> p q x", q=nq), in_=wv[:, q0 : q0 + nq, :])
+            wv = W[i, j].rearrange("(p t) a -> p (t a)", t=16)
+            nc.sync.dma_start(out=raw[:], in_=wv[:, q0 * 4 * A : (q0 + nq) * 4 * A])
             for c in range(nq):
                 src[(i, j, q0 + c)] = (raw[:].bitcast(F32), c * 2 * A, A // 2)
 
         load_w(2, 2, 0, 1, const, "rawh0")
         load_w(2, 2, 1, 1, const, "rawh1")
         load_w(2, 2, 2, 2, rawp, "raw")
+        load_w(1, 1, 0, 2, rawp, "raw")
+        load_w(2, 1, 0, 2, rawp, "raw")
         g01raw = const.tile([P, NT * 2 * A], BF16, name="g01raw")
         nc.sync.dma_start(
             out=g01raw[:].rearrange("p (t i a) -> p t i a", t=NT, i=2), in_=gv[:, :, 0:2, :]
         )
         for i in range(2):
             src[("g", i)] = (g01raw[:].bitcast(F32), i * (A // 2), A)
-        for j, h in ((1, 0), (1, 1), (0, 0), (0, 1)):
+        for j, h in ((1, 1), (0, 0), (0, 1)):
             for i in range(j, L):
                 load_w(i, j, 2 * h, 2, rawp, "raw")
 
@@ -112,17 +114,21 @@ def tile_decoder_kernel(tc, x, W, grad_out, out):
                 prev = key
             quantise_chunk(prev)
 
-        def keys_of(j, h):
-            return [(i, j, q) for q in (2 * h, 2 * h + 1) for i in range(j, L)]
+        def keys_of(j, qs):
+            return [(i, j, q) for q in qs for i in range(j, L)]
 
-        def run_m(j, h):
+        rows = {}
+
+        def run_m(j, qs):
             for t in range(NT):
-                ot = outp.tile([P, 2 * CH], F32, name="ot")
-                for c in range(2):
+                if (t, j) not in rows:
+                    rows[(t, j)] = outp.tile([P, F], F32, name="ot")
+                ot = rows[(t, j)]
+                for q in qs:
                     acc = psum.tile([P, 512], F32, name="acc", tag="bank")
                     for i in range(j, L):
                         gc, gs = codes[("g", i)]
-                        wc, ws = codes[(i, j, 2 * h + c)]
+                        wc, ws = codes[(i, j, q)]
                         nc.tensor.matmul_mx(
                             out=acc[:],
                             lhsT=gc[:, t * P : (t + 1) * P].bitcast(E5X4),
@@ -133,22 +139,21 @@ def tile_decoder_kernel(tc, x, W, grad_out, out):
                             stop=(i == L - 1),
                         )
                     copy_out(
-                        count["ev"] % 2 == 1,
-                        ot[:, c * CH : (c + 1) * CH].rearrange("p (f s) -> p f s", s=4),
+                        (count["ev"] // 2) % 2 == 1,
+                        ot[:].rearrange("p (f q s) -> p q f s", q=NQ, s=4)[:, q],
                         acc[:].rearrange("p (s f) -> p f s", s=4),
                     )
                     count["ev"] += 1
-                nc.sync.dma_start(out=ov[:, t, j, h * 2 * CH : (h + 1) * 2 * CH], in_=ot[:])
+                if qs[-1] == NQ - 1:
+                    nc.sync.dma_start(out=ov[:, t, j, :], in_=ot[:])
 
-        run_t([("g", 2)] + keys_of(2, 0))
-        run_t(keys_of(2, 1))
-        run_m(2, 0)
-        run_t([("g", 1), ("g", 0)] + keys_of(1, 0))
-        run_m(2, 1)
-        run_t(keys_of(1, 1))
-        run_m(1, 0)
-        run_t(keys_of(0, 0))
-        run_m(1, 1)
-        run_t(keys_of(0, 1))
-        run_m(0, 0)
-        run_m(0, 1)
+        run_t([("g", 2)] + keys_of(2, (0, 1)))
+        run_m(2, (0, 1))
+        run_t(keys_of(2, (2, 3)) + keys_of(1, (0, 1)))
+        run_m(2, (2, 3))
+        run_t([("g", 1), ("g", 0)] + keys_of(1, (2, 3)))
+        run_m(1, (0, 1))
+        run_t(keys_of(0, (0, 1)))
+        run_m(1, (2, 3))
+        run_t(keys_of(0, (2, 3)))
+        run_m(0, (0, 1, 2, 3))

@@ -27,7 +27,7 @@ def tile_decoder_kernel(tc, x, W, grad_out, out):
         rawp = ctx.enter_context(tc.tile_pool(name="rawp", bufs=6))
         grp = ctx.enter_context(tc.tile_pool(name="grp", bufs=4))
         cod = ctx.enter_context(tc.tile_pool(name="cod", bufs=12))
-        outp = ctx.enter_context(tc.tile_pool(name="outp", bufs=12))
+        outp = ctx.enter_context(tc.tile_pool(name="outp", bufs=8))
         psum = ctx.enter_context(tc.psum_pool(name="psum", bufs=8))
 
         ident = const.tile([P, P], F32, name="ident")
@@ -43,8 +43,12 @@ def tile_decoder_kernel(tc, x, W, grad_out, out):
 
         def load_w(i, j, q0, nq, pool, tag):
             raw = pool.tile([P, nq * 4 * A], BF16, name="raw%d%d%d" % (i, j, q0), tag=tag)
-            wv = W[i, j].rearrange("(p t) a -> p (t a)", t=16)
-            nc.sync.dma_start(out=raw[:], in_=wv[:, q0 * 4 * A : (q0 + nq) * 4 * A])
+            if j == 0:
+                wv = W[i, j].rearrange("(h p t) a -> h p (t a)", p=P, t=8)
+                nc.sync.dma_start(out=raw[:], in_=wv[q0 // 2])
+            else:
+                wv = W[i, j].rearrange("(p t) a -> p (t a)", t=16)
+                nc.sync.dma_start(out=raw[:], in_=wv[:, q0 * 4 * A : (q0 + nq) * 4 * A])
             for c in range(nq):
                 src[(i, j, q0 + c)] = (raw[:].bitcast(F32), c * 2 * A, A // 2)
 
@@ -121,9 +125,14 @@ def tile_decoder_kernel(tc, x, W, grad_out, out):
 
         def run_m(j, qs):
             for t in range(NT):
-                if (t, j) not in rows:
-                    rows[(t, j)] = outp.tile([P, F], F32, name="ot")
-                ot = rows[(t, j)]
+                if j == 0:
+                    ot = outp.tile([P, F // 2], F32, name="oh")
+                    views = ot[:].rearrange("p (f c s) -> p c f s", c=2, s=4)
+                else:
+                    if (t, j) not in rows:
+                        rows[(t, j)] = outp.tile([P, F], F32, name="ot")
+                    ot = rows[(t, j)]
+                    views = ot[:].rearrange("p (f q s) -> p q f s", q=NQ, s=4)
                 for q in qs:
                     acc = psum.tile([P, 512], F32, name="acc", tag="bank")
                     for i in range(j, L):
@@ -140,11 +149,14 @@ def tile_decoder_kernel(tc, x, W, grad_out, out):
                         )
                     copy_out(
                         (count["ev"] // 2) % 2 == 1,
-                        ot[:].rearrange("p (f q s) -> p q f s", q=NQ, s=4)[:, q],
+                        views[:, q % 2 if j == 0 else q],
                         acc[:].rearrange("p (s f) -> p f s", s=4),
                     )
                     count["ev"] += 1
-                if qs[-1] == NQ - 1:
+                if j == 0:
+                    h = qs[0] // 2
+                    nc.sync.dma_start(out=ov[:, t, j, h * (F // 2) : (h + 1) * (F // 2)], in_=ot[:])
+                elif qs[-1] == NQ - 1:
                     nc.sync.dma_start(out=ov[:, t, j, :], in_=ot[:])
 
         run_t([("g", 2)] + keys_of(2, (0, 1)))
@@ -156,4 +168,5 @@ def tile_decoder_kernel(tc, x, W, grad_out, out):
         run_t(keys_of(0, (0, 1)))
         run_m(1, (2, 3))
         run_t(keys_of(0, (2, 3)))
-        run_m(0, (0, 1, 2, 3))
+        run_m(0, (0, 1))
+        run_m(0, (2, 3))

@@ -27,19 +27,21 @@ def tile_decoder_kernel(tc, x, W, grad_out, out):
         rawp = ctx.enter_context(tc.tile_pool(name="rawp", bufs=6))
         grp = ctx.enter_context(tc.tile_pool(name="grp", bufs=4))
         cod = ctx.enter_context(tc.tile_pool(name="cod", bufs=12))
-        outp = ctx.enter_context(tc.tile_pool(name="outp", bufs=8))
+        outp = ctx.enter_context(tc.tile_pool(name="outp", bufs=12))
         psum = ctx.enter_context(tc.psum_pool(name="psum", bufs=8))
 
         ident = const.tile([P, P], F32, name="ident")
         make_identity(nc, ident[:])
 
-        gv = grad_out.rearrange("(p t) i a -> p t i a", t=NT)
+        gv = grad_out.rearrange("(p t) i a -> p (t i a)", t=NT)
         ov = out.rearrange("(m t) j f -> m t j f", t=NT)
 
         src = {}
-        g2raw = const.tile([P, NT * A], BF16, name="g2raw")
-        nc.sync.dma_start(out=g2raw[:].rearrange("p (t a) -> p t a", t=NT), in_=gv[:, :, 2, :])
-        src[("g", 2)] = (g2raw[:].bitcast(F32), 0, A // 2)
+        for hb in range(2):
+            graw = const.tile([P, 2 * L * A], BF16, name="graw%d" % hb)
+            nc.sync.dma_start(out=graw[:], in_=gv[:, hb * 2 * L * A : (hb + 1) * 2 * L * A])
+            for i in range(L):
+                src[("g", i, hb)] = (graw[:].bitcast(F32), i * (A // 2), L * A // 2)
 
         def load_w(i, j, q0, nq, pool, tag):
             raw = pool.tile([P, nq * 4 * A], BF16, name="raw%d%d%d" % (i, j, q0), tag=tag)
@@ -57,12 +59,6 @@ def tile_decoder_kernel(tc, x, W, grad_out, out):
         load_w(2, 2, 2, 2, rawp, "raw")
         load_w(1, 1, 0, 2, rawp, "raw")
         load_w(2, 1, 0, 2, rawp, "raw")
-        g01raw = const.tile([P, NT * 2 * A], BF16, name="g01raw")
-        nc.sync.dma_start(
-            out=g01raw[:].rearrange("p (t i a) -> p t i a", t=NT, i=2), in_=gv[:, :, 0:2, :]
-        )
-        for i in range(2):
-            src[("g", i)] = (g01raw[:].bitcast(F32), i * (A // 2), A)
         for j, h in ((1, 1), (0, 0), (0, 1)):
             for i in range(j, L):
                 load_w(i, j, 2 * h, 2, rawp, "raw")
@@ -70,6 +66,10 @@ def tile_decoder_kernel(tc, x, W, grad_out, out):
         count = {"tc": 0, "ev": 0}
         grouped = {}
         codes = {}
+        for i in range(L):
+            gcw = const.tile([P, CH], U32, name="gcodes%d" % i, align_bytes=64)
+            gsc = const.tile([P, CH], U8, name="gscale%d" % i, align_bytes=64)
+            codes[("g", i)] = (gcw, gsc)
 
         def copy_out(turn_vector, dst, srcv):
             if turn_vector:
@@ -79,10 +79,13 @@ def tile_decoder_kernel(tc, x, W, grad_out, out):
 
         def transpose_chunk(key):
             words, col0, step = src[key]
-            g = grp.tile([P, 4 * CH], BF16, name="grouped", align_bytes=64)
+            if key[0] == "g":
+                g = grp.tile([P, 2 * CH], BF16, name="ggrouped", align_bytes=64)
+            else:
+                g = grp.tile([P, 4 * CH], BF16, name="grouped", align_bytes=64)
             grouped[key] = g
             gf = g[:].bitcast(F32)
-            for h in range(2):
+            for h in range(1 if key[0] == "g" else 2):
                 xt = psum.tile([P, 512], F32, name="xt", tag="bank")
                 for u in range(2):
                     for s in range(2):
@@ -99,15 +102,14 @@ def tile_decoder_kernel(tc, x, W, grad_out, out):
 
         def quantise_chunk(key):
             if key[0] == "g":
-                cw = const.tile([P, CH], U32, name="gcodes%d" % key[1], align_bytes=64)
-                sc = const.tile([P, CH], U8, name="gscale%d" % key[1], align_bytes=64)
-                fmt = E5X4
+                gcw, gsc = codes[("g", key[1])]
+                cols = slice(key[2] * 2 * P, (key[2] + 1) * 2 * P)
+                nc.vector.quantize_mx(out=gcw[:, cols].bitcast(E5X4), scales=gsc[:, cols], in_=grouped[key][:])
             else:
                 cw = cod.tile([P, CH], U32, name="wcodes", align_bytes=64)
                 sc = cod.tile([P, CH], U8, name="wscale", align_bytes=64)
-                fmt = E4X4
-            nc.vector.quantize_mx(out=cw[:].bitcast(fmt), scales=sc[:], in_=grouped[key][:])
-            codes[key] = (cw, sc)
+                nc.vector.quantize_mx(out=cw[:].bitcast(E4X4), scales=sc[:], in_=grouped[key][:])
+                codes[key] = (cw, sc)
 
         def run_t(keys):
             prev = None
@@ -125,14 +127,9 @@ def tile_decoder_kernel(tc, x, W, grad_out, out):
 
         def run_m(j, qs):
             for t in range(NT):
-                if j == 0:
-                    ot = outp.tile([P, F // 2], F32, name="oh")
-                    views = ot[:].rearrange("p (f c s) -> p c f s", c=2, s=4)
-                else:
-                    if (t, j) not in rows:
-                        rows[(t, j)] = outp.tile([P, F], F32, name="ot")
-                    ot = rows[(t, j)]
-                    views = ot[:].rearrange("p (f q s) -> p q f s", q=NQ, s=4)
+                if (t, j) not in rows:
+                    rows[(t, j)] = outp.tile([P, F], F32, name="ot")
+                ot = rows[(t, j)]
                 for q in qs:
                     acc = psum.tile([P, 512], F32, name="acc", tag="bank")
                     for i in range(j, L):
@@ -147,26 +144,29 @@ def tile_decoder_kernel(tc, x, W, grad_out, out):
                             start=(i == j),
                             stop=(i == L - 1),
                         )
+                    if j == 0:
+                        dst = ot[:].rearrange("p (h f c s) -> p h c f s", h=2, c=2, s=4)[:, q // 2, q % 2]
+                    else:
+                        dst = ot[:].rearrange("p (f q s) -> p q f s", q=NQ, s=4)[:, q]
                     copy_out(
                         (count["ev"] // 2) % 2 == 1,
-                        views[:, q % 2 if j == 0 else q],
+                        dst,
                         acc[:].rearrange("p (s f) -> p f s", s=4),
                     )
                     count["ev"] += 1
-                if j == 0:
-                    h = qs[0] // 2
-                    nc.sync.dma_start(out=ov[:, t, j, h * (F // 2) : (h + 1) * (F // 2)], in_=ot[:])
-                elif qs[-1] == NQ - 1:
+                    if j == 0 and t == NT - 1 and q % 2 == 1:
+                        half = slice((q // 2) * (F // 2), (q // 2 + 1) * (F // 2))
+                        nc.sync.dma_start(out=ov[:, t, j, half], in_=ot[:, half])
+                if qs[-1] == NQ - 1 and not (j == 0 and t == NT - 1):
                     nc.sync.dma_start(out=ov[:, t, j, :], in_=ot[:])
 
-        run_t([("g", 2)] + keys_of(2, (0, 1)))
+        run_t([("g", i, hb) for hb in range(2) for i in (2, 1, 0)] + keys_of(2, (0, 1)))
         run_m(2, (0, 1))
         run_t(keys_of(2, (2, 3)) + keys_of(1, (0, 1)))
         run_m(2, (2, 3))
-        run_t([("g", 1), ("g", 0)] + keys_of(1, (2, 3)))
+        run_t(keys_of(1, (2, 3)))
         run_m(1, (0, 1))
         run_t(keys_of(0, (0, 1)))
         run_m(1, (2, 3))
         run_t(keys_of(0, (2, 3)))
-        run_m(0, (0, 1))
-        run_m(0, (2, 3))
+        run_m(0, (0, 1, 2, 3))

from contextlib import ExitStack

import concourse.mybir as mybir
from concourse.masks import make_identity

F32 = mybir.dt.float32
BF16 = mybir.dt.bfloat16
U32 = mybir.dt.uint32
U8 = mybir.dt.uint8
E4X4 = mybir.dt.float8_e4m3fn_x4
E5X4 = mybir.dt.float8_e5m2_x4

P = 128
B, L, F, A = 512, 3, 2048, 512
NT = B // P
CH = 512
NQ = F // CH
FLOPS = 2 * B * A * F * 6
BYTES = 6 * F * A * 2 + B * L * A * 2 + B * L * F * 4


def tile_decoder_kernel(tc, x, W, grad_out, out):
    nc = tc.nc
    with ExitStack() as ctx:
        ctx.enter_context(tc.manual_schedule())
        const = ctx.enter_context(tc.tile_pool(name="const", bufs=1))
        rawp = ctx.enter_context(tc.tile_pool(name="rawp", bufs=6))
        grp = ctx.enter_context(tc.tile_pool(name="grp", bufs=4))
        cod = ctx.enter_context(tc.tile_pool(name="cod", bufs=12))
        outp = ctx.enter_context(tc.tile_pool(name="outp", bufs=12))
        psum = ctx.enter_context(tc.psum_pool(name="psum", bufs=8))

        ident = const.tile([P, P], F32, name="ident")
        make_identity(nc, ident[:])

        gv = grad_out.rearrange("(p t) i a -> p (t i a)", t=NT)
        ov = out.rearrange("(m t) j f -> m t j f", t=NT)

        src = {}
        for hb in range(2):
            graw = const.tile([P, 2 * L * A], BF16, name="graw%d" % hb)
            nc.sync.dma_start(out=graw[:], in_=gv[:, hb * 2 * L * A : (hb + 1) * 2 * L * A])
            for i in range(L):
                src[("g", i, hb)] = (graw[:].bitcast(F32), i * (A // 2), L * A // 2)

        def load_w(i, j, q0, nq, pool, tag):
            raw = pool.tile([P, nq * 4 * A], BF16, name="raw%d%d%d" % (i, j, q0), tag=tag)
            if j == 0:
                wv = W[i, j].rearrange("(h p t) a -> h p (t a)", p=P, t=8)
                nc.sync.dma_start(out=raw[:], in_=wv[q0 // 2])
            else:
                wv = W[i, j].rearrange("(p t) a -> p (t a)", t=16)
                nc.sync.dma_start(out=raw[:], in_=wv[:, q0 * 4 * A : (q0 + nq) * 4 * A])
            for c in range(nq):
                src[(i, j, q0 + c)] = (raw[:].bitcast(F32), c * 2 * A, A // 2)

        load_w(2, 2, 0, 1, const, "rawh0")
        load_w(2, 2, 1, 1, const, "rawh1")
        load_w(2, 2, 2, 2, rawp, "raw")
        load_w(1, 1, 0, 2, rawp, "raw")
        load_w(2, 1, 0, 2, rawp, "raw")
        for j, h in ((1, 1), (0, 0), (0, 1)):
            for i in range(j, L):
                load_w(i, j, 2 * h, 2, rawp, "raw")

        count = {"tc": 0, "ev": 0}
        grouped = {}
        codes = {}
        for i in range(L):
            gcw = const.tile([P, CH], U32, name="gcodes%d" % i, align_bytes=64)
            gsc = const.tile([P, CH], U8, name="gscale%d" % i, align_bytes=64)
            codes[("g", i)] = (gcw, gsc)

        def copy_out(turn_vector, dst, srcv):
            if turn_vector:
                nc.vector.tensor_copy(out=dst, in_=srcv)
            else:
                nc.scalar.copy(out=dst, in_=srcv)

        def transpose_chunk(key):
            words, col0, step = src[key]
            if key[0] == "g":
                g = grp.tile([P, 2 * CH], BF16, name="ggrouped", align_bytes=64)
            else:
                g = grp.tile([P, 4 * CH], BF16, name="grouped", align_bytes=64)
            grouped[key] = g
            gf = g[:].bitcast(F32)
            for h in range(1 if key[0] == "g" else 2):
                xt = psum.tile([P, 512], F32, name="xt", tag="bank")
                for u in range(2):
                    for s in range(2):
                        c = col0 + (2 * h + s) * step + u * P
                        nc.tensor.transpose(
                            xt[:, u * 256 + s * P : u * 256 + (s + 1) * P], words[:, c : c + P], ident[:]
                        )
                copy_out(
                    count["tc"] % 4 == 3,
                    gf[:, h * 512 : (h + 1) * 512].rearrange("p (c u) -> p c u", u=2),
                    xt[:].rearrange("p (u c) -> p c u", u=2),
                )
                count["tc"] += 1

        def quantise_chunk(key):
            if key[0] == "g":
                gcw, gsc = codes[("g", key[1])]
                cols = slice(key[2] * 2 * P, (key[2] + 1) * 2 * P)
                nc.vector.quantize_mx(out=gcw[:, cols].bitcast(E5X4), scales=gsc[:, cols], in_=grouped[key][:])
            else:
                cw = cod.tile([P, CH], U32, name="wcodes", align_bytes=64)
                sc = cod.tile([P, CH], U8, name="wscale", align_bytes=64)
                nc.vector.quantize_mx(out=cw[:].bitcast(E4X4), scales=sc[:], in_=grouped[key][:])
                codes[key] = (cw, sc)

        def run_t(keys):
            prev = None
            for key in keys:
                transpose_chunk(key)
                if prev is not None:
                    quantise_chunk(prev)
                prev = key
            quantise_chunk(prev)

        def keys_of(j, qs):
            return [(i, j, q) for q in qs for i in range(j, L)]

        rows = {}

        def run_m(j, qs):
            for t in range(NT):
                if (t, j) not in rows:
                    rows[(t, j)] = outp.tile([P, F], F32, name="ot")
                ot = rows[(t, j)]
                for q in qs:
                    acc = psum.tile([P, 512], F32, name="acc", tag="bank")
                    for i in range(j, L):
                        gc, gs = codes[("g", i)]
                        wc, ws = codes[(i, j, q)]
                        nc.tensor.matmul_mx(
                            out=acc[:],
                            lhsT=gc[:, t * P : (t + 1) * P].bitcast(E5X4),
                            lhsT_scale=gs[:, t * P : (t + 1) * P],
                            rhs=wc[:].bitcast(E4X4),
                            rhs_scale=ws[:],
                            start=(i == j),
                            stop=(i == L - 1),
                        )
                    if j == 0:
                        dst = ot[:].rearrange("p (h f c s) -> p h c f s", h=2, c=2, s=4)[:, q // 2, q % 2]
                    else:
                        dst = ot[:].rearrange("p (f q s) -> p q f s", q=NQ, s=4)[:, q]
                    copy_out(
                        (count["ev"] // 2) % 2 == 1,
                        dst,
                        acc[:].rearrange("p (s f) -> p f s", s=4),
                    )
                    count["ev"] += 1
                    if j == 0 and t == NT - 1 and q % 2 == 1:
                        half = slice((q // 2) * (F // 2), (q // 2 + 1) * (F // 2))
                        nc.sync.dma_start(out=ov[:, t, j, half], in_=ot[:, half])
                if qs[-1] == NQ - 1 and not (j == 0 and t == NT - 1):
                    nc.sync.dma_start(out=ov[:, t, j, :], in_=ot[:])

        run_t([("g", i, hb) for hb in range(2) for i in (2, 1, 0)] + keys_of(2, (0, 1)))
        run_m(2, (0, 1))
        run_t(keys_of(2, (2, 3)) + keys_of(1, (0, 1)))
        run_m(2, (2, 3))
        run_t(keys_of(1, (2, 3)))
        run_m(1, (0, 1))
        run_t(keys_of(0, (0, 1)))
        run_m(1, (2, 3))
        run_t(keys_of(0, (2, 3)))
        run_m(0, (0, 1, 2, 3))
